import numpy as np
import ml_dtypes


def mxq(x, axis, fmt="e4m3"):
    dtype, down = {"e4m3": (ml_dtypes.float8_e4m3fn, 7), "e5m2": (ml_dtypes.float8_e5m2, 14)}[fmt]
    v = np.moveaxis(np.asarray(x, np.float32).astype(ml_dtypes.bfloat16).astype(np.float64), axis, -1)
    blocks = v.reshape(v.shape[:-1] + (-1, 32))
    amax = np.abs(blocks).max(-1, keepdims=True)
    byte = np.maximum(np.where(amax > 0, np.frexp(amax)[1] - 1 + 127, 0) - down, 1)
    scale = np.exp2(byte - 127.0)
    codes = (blocks / scale).astype(np.float32).astype(dtype).astype(np.float64)
    return np.moveaxis((codes * scale).reshape(v.shape), -1, axis)


WIDE = False


def mx_kscale(k):
    if not WIDE:
        return np.ones(k)
    levels = np.array([10, -10, 5, -5, 0])
    a = np.random.permutation(np.resize(levels, k // 512 * 4)).reshape(k // 512, 4)
    idx = np.arange(k)
    return np.exp2(a[idx // 512, idx % 128 // 32])


BF16 = ml_dtypes.bfloat16


def bf(x):
    return np.asarray(x, np.float32).astype(BF16)


def f64(x):
    return np.asarray(x).astype(np.float64)


E2M1 = np.array([0.0, 0.5, 1.0, 1.5, 2.0, 3.0, 4.0, 6.0, -0.0, -0.5, -1.0, -1.5, -2.0, -3.0, -4.0, -6.0])


def pack_weight(w, fmt):
    k, n = w.shape
    w = f64(bf(w)).reshape(k // 32, 32, n)
    amax = np.abs(w).max(1)
    if fmt == "e4m3":
        byte = np.frexp(amax)[1] - 1 + 127 - 7
    else:
        mant, ex = np.frexp(amax / 6.0)
        byte = np.where(mant > 0.5, ex, ex - 1) + 127
    byte = np.clip(np.where(amax > 0, byte, 1), 1, 254)
    scaled = (w * np.exp2(127.0 - byte)[:, None, :]).reshape(k, n).astype(np.float32)
    by_word = np.ascontiguousarray(scaled.reshape(k // 512, 128, 4, n).transpose(0, 1, 3, 2))
    if fmt == "e4m3":
        words = by_word.astype(ml_dtypes.float8_e4m3fn).view(np.uint8)
    else:
        c = by_word.astype(ml_dtypes.float4_e2m1fn).view(np.uint8) & 0xF
        words = c[..., 0::2] | (c[..., 1::2] << 4)
    return np.ascontiguousarray(words), np.ascontiguousarray(byte.astype(np.uint8).reshape(k // 512, 16, n))


def unpack_weight(words, scales, fmt):
    g, p, n, _ = words.shape
    if fmt == "e4m3":
        vals = np.ascontiguousarray(words).view(ml_dtypes.float8_e4m3fn).astype(np.float64)
    else:
        nib = np.empty((g, p, n, 4), np.uint8)
        nib[..., 0::2] = words & 0xF
        nib[..., 1::2] = words >> 4
        vals = E2M1[nib]
    vals = vals * np.repeat(np.exp2(scales.astype(np.float64) - 127.0), 8, axis=1)[..., None]
    return vals.transpose(0, 1, 3, 2).reshape(g * 512, n)

def pack4(w):
    words, scales = pack_weight(w, "e2m1")
    return words.reshape(words.shape[0], 128, -1), scales


def unpack4(words, scales):
    return unpack_weight(words.reshape(words.shape[0], 128, -1, 2), scales, "e2m1")


B, H, L, E, QD = 64, 1, 128, 1024, 128
EPS = 1e-5


def build_decay_mask(num_heads, max_len):
    r = f64(np.arange(max_len))
    dec = np.array([1.0 - 2.0 ** (-5 - h) for h in range(num_heads)])
    expo = r[None, :] - r[:, None]
    return np.where(r[:, None] >= r[None, :], dec[:, None, None] ** expo[None], 0.0)


def setup_inputs():
    s = mx_kscale(E)
    kv = (0.1 + 0.32 * np.random.standard_normal((B, H, L, QD))) * (0.1 + 0.32 * np.random.standard_normal((B, H, L, QD)))
    x = bf(np.random.standard_normal((B, H, L, E)) * s)
    Wq = np.random.standard_normal((QD, E)) / np.sqrt(E) / s
    Wq_words, Wq_scales = pack4(np.ascontiguousarray(Wq.T))
    return {"x": x,
            "Wq_words": Wq_words,
            "Wq_scales": Wq_scales,
            "bq": bf(0.3 + 0.3 * np.random.standard_normal(QD)),
            "kv": bf(kv),
            "decay_mask": bf(build_decay_mask(H, L))}


def reference(x, Wq_words, Wq_scales, bq, kv, decay_mask):
    b, h, l, e = x.shape
    Q = (mxq(f64(x), 3, "e4m3") @ unpack4(Wq_words, Wq_scales)) + f64(bq)
    D = f64(decay_mask)[0, :l, :l]
    y = Q * (f64(kv) @ D.T)
    mean = y.mean(axis=(2, 3), keepdims=True)
    var = ((y - mean) ** 2).mean(axis=(2, 3), keepdims=True)
    y = (y - mean) / np.sqrt(var + EPS)
    return y.reshape(b, l, -1)

@@ -1,0 +1,221 @@
+from contextlib import ExitStack
+
+import concourse.mybir as mybir
+from concourse.masks import make_identity
+
+F32 = mybir.dt.float32
+BF16 = mybir.dt.bfloat16
+I32 = mybir.dt.int32
+U32 = mybir.dt.uint32
+U8 = mybir.dt.uint8
+FP8X4 = mybir.dt.float8_e4m3fn_x4
+FP4X4 = mybir.dt.float4_e2m1fn_x4
+ALU = mybir.AluOpType
+ACT = mybir.ActivationFunctionType
+
+P = 128
+SAMPLES = 64
+L = 128
+E = 1024
+QD = 128
+EPS = 1e-5
+K_PASS = 512
+PASSES = E // K_PASS
+WORDS_PASS = K_PASS // 2
+S = 4
+GROUP_ROWS = P * S
+GROUPS = SAMPLES * L // GROUP_ROWS
+KV_CHUNK = 4
+
+FLOPS = 2 * SAMPLES * L * E * QD + 2 * SAMPLES * L * QD * QD
+
+
+def tile_parallelretention_pb_t_kernel(tc, x, Wq_words, Wq_scales, bq, kv, decay_mask, out):
+    nc = tc.nc
+    x_view = x.rearrange("b h l e -> (b h l) e").rearrange("(g p j) e -> g p j e", p=P, j=S)
+    kv_view = kv.rearrange("b h l k -> (b h l) k").rearrange("(g p j) k -> p g (j k)", p=P, j=S)
+    out_view = out.rearrange("b l q -> (b l) q").rearrange("(g p j) q -> g p (j q)", p=P, j=S)
+
+    with ExitStack() as ctx:
+        ctx.enter_context(tc.manual_schedule())
+        const = ctx.enter_context(tc.tile_pool(name="const", bufs=1))
+        x_pool = ctx.enter_context(tc.tile_pool(name="x_pool", bufs=GROUPS))
+        kv_pool = ctx.enter_context(tc.tile_pool(name="kv_pool", bufs=GROUPS // KV_CHUNK))
+        two = ctx.enter_context(tc.tile_pool(name="two", bufs=2))
+        four = ctx.enter_context(tc.tile_pool(name="four", bufs=4))
+        psum_x = ctx.enter_context(tc.psum_pool(name="psum_x", bufs=S))
+        psum_one = ctx.enter_context(tc.psum_pool(name="psum_one", bufs=1))
+
+        w_planes = const.tile([P, PASSES, QD], U8, align_bytes=64)
+        nc.vector.memset(w_planes[:].bitcast(I32), 0)
+        eps = const.tile([P, 1], F32)
+        nc.vector.memset(eps[:], EPS)
+        sample_mean = const.tile([P, P], F32)
+        nc.vector.memset(sample_mean[:], 0.0)
+        for a in range(P // 32):
+            rows = slice(32 * a, 32 * a + 32)
+            nc.vector.memset(sample_mean[rows, rows], 1.0 / (L * QD))
+        warm = const.tile([P, 1], F32)
+        nc.scalar.activation(out=warm[:], in_=eps[:], func=ACT.Sqrt)
+        ident_f32 = const.tile([P, P], F32)
+        make_identity(nc, ident_f32[:])
+        ident_bf16 = const.tile([P, P], BF16)
+        make_identity(nc, ident_bf16[:])
+
+        d_sb = const.tile([P, P], BF16)
+        nc.scalar.dma_start(out=d_sb[:], in_=decay_mask.rearrange("o q k -> (o q) k"))
+        bq_bf16 = const.tile([P, QD], BF16)
+        nc.scalar.dma_start(out=bq_bf16[:], in_=bq.partition_broadcast(P))
+
+        x_tiles = []
+        kv_tiles = []
+        w_words = const.tile([P, PASSES, 2 * QD], U8, align_bytes=64)
+        for g in range(GROUPS):
+            x_sb = x_pool.tile([P, S, E], BF16)
+            nc.sync.dma_start(out=x_sb[:], in_=x_view[g])
+            x_tiles.append(x_sb)
+            if g == 0:
+                nc.sync.dma_start(
+                    out=w_words[:].bitcast(I32), in_=Wq_words.bitcast(I32).rearrange("c p n -> p c n")
+                )
+                for quad in range(4):
+                    nc.sync.dma_start(
+                        out=w_planes[32 * quad : 32 * quad + 4].bitcast(I32),
+                        in_=Wq_scales.bitcast(I32)[:, 4 * quad : 4 * quad + 4, :].rearrange("c r n -> r c n"),
+                    )
+            if g % KV_CHUNK == 0:
+                kv_sb = kv_pool.tile([P, KV_CHUNK, S * QD], BF16)
+                nc.sync.dma_start(out=kv_sb[:], in_=kv_view[:, g : g + KV_CHUNK, :])
+                kv_tiles.append(kv_sb)
+
+        bias = const.tile([P, QD], F32)
+        nc.vector.tensor_copy(out=bias[:], in_=bq_bf16[:])
+        dT_ps = psum_one.tile([P, S, P], BF16, name="kvT_ps")
+        nc.tensor.transpose(dT_ps[:, 0, :], d_sb[:], ident_bf16[:])
+        dT = const.tile([P, QD], BF16)
+        nc.vector.tensor_copy(out=dT[:], in_=dT_ps[:, 0, :])
+
+        live = {}
+
+        def transpose_and_quantise(g):
+            grouped = two.tile([P, S, PASSES, P, 4], BF16, align_bytes=64)
+            codes = two.tile([P, S, PASSES, P], U32, align_bytes=64)
+            planes = two.tile([P, S, PASSES, P], U8, align_bytes=64)
+            for j in range(S):
+                xT_ps = psum_x.tile([P, PASSES, 2, P], F32)
+                words = x_tiles[g][:, j, :].bitcast(F32)
+                for c in range(PASSES):
+                    for u in range(2):
+                        nc.tensor.transpose(
+                            xT_ps[:, c, u, :],
+                            words[:, WORDS_PASS * c + u : WORDS_PASS * (c + 1) : 2],
+                            ident_f32[:],
+                        )
+                nc.scalar.copy(out=grouped[:, j].bitcast(F32), in_=xT_ps[:].rearrange("p c u r -> p c r u"))
+            kvT_ps = psum_one.tile([P, S, P], BF16)
+            kv_sb = kv_tiles[g // KV_CHUNK]
+            for j in range(S):
+                nc.tensor.transpose(kvT_ps[:, j, :], kv_sb[:, g % KV_CHUNK, QD * j : QD * (j + 1)], ident_bf16[:])
+            for half in range(2):
+                blocks = slice(2 * half, 2 * half + 2)
+                if half == 1:
+                    kvT = two.tile([P, S, P], BF16)
+                    nc.vector.tensor_copy(out=kvT[:], in_=kvT_ps[:])
+                nc.vector.quantize_mx(
+                    out=codes[:, blocks].rearrange("p j c r -> p (j c r)").bitcast(FP8X4),
+                    scales=planes[:, blocks].rearrange("p j c r -> p (j c r)"),
+                    in_=grouped[:, blocks].rearrange("p j c r t -> p (j c r t)"),
+                )
+            live[("codes", g)] = (codes, planes, kvT)
+
+        def multiply(g):
+            codes, planes, kvT = live.pop(("codes", g))
+            q_ps = psum_one.tile([P, S, QD], F32)
+            g_ps = psum_one.tile([P, S, QD], F32)
+            for j in range(S):
+                for c in range(PASSES):
+                    nc.tensor.matmul_mx(
+                        out=q_ps[:, j, :],
+                        lhsT=codes[:, j, c, :].bitcast(FP8X4),
+                        lhsT_scale=planes[:, j, c, :],
+                        rhs=w_words[:, c, :].bitcast(FP4X4),
+                        rhs_scale=w_planes[:, c, :],
+                        start=(c == 0),
+                        stop=(c == PASSES - 1),
+                    )
+            for j in range(S):
+                nc.tensor.matmul(out=g_ps[:, j, :], lhsT=kvT[:, j, :], rhs=dT[:], start=True, stop=True)
+            live[("qg", g)] = (q_ps, g_ps)
+
+        def product(g):
+            q_ps, g_ps = live.pop(("qg", g))
+            biased = two.tile([P, S, QD], F32)
+            nc.vector.tensor_tensor(
+                out=biased[:], in0=q_ps[:], in1=bias[:].unsqueeze(1).to_broadcast([P, S, QD]), op=ALU.add
+            )
+            y = four.tile([P, S * QD], F32)
+            sums = four.tile([P, 2, 8], F32)
+            nc.vector.scalar_tensor_tensor(
+                out=y[:],
+                in0=g_ps[:].rearrange("p j q -> p (j q)"),
+                scalar=1.0,
+                in1=biased[:].rearrange("p j q -> p (j q)"),
+                op0=ALU.mult,
+                op1=ALU.mult,
+                accum_out=sums[:, 0, 0:1],
+            )
+            live[("y", g)] = (y, sums)
+
+        def sum_of_squares(g):
+            y, sums = live[("y", g)]
+            squares = two.tile([P, S * QD], F32)
+            nc.scalar.activation(out=squares[:], in_=y[:], func=ACT.Square, accum_out=sums[:, 1, 0:1])
+
+        def sample_statistics(g):
+            y, sums = live[("y", g)]
+            stat_ps = psum_one.tile([P, 2], F32)
+            nc.tensor.matmul(out=stat_ps[:], lhsT=sample_mean[:], rhs=sums[:, :, 0], start=True, stop=True)
+            live[("stat", g)] = stat_ps
+
+        def deviation(g):
+            stat_ps = live[("stat", g)]
+            minus_var = two.tile([P, 1], F32)
+            nc.vector.tensor_scalar(
+                out=minus_var[:],
+                in0=stat_ps[:, 0:1],
+                scalar1=stat_ps[:, 0:1],
+                scalar2=stat_ps[:, 1:2],
+                op0=ALU.mult,
+                op1=ALU.subtract,
+            )
+            std = two.tile([P, 1], F32)
+            nc.scalar.activation(out=std[:], in_=minus_var[:], func=ACT.Sqrt, bias=eps[:], scale=-1.0)
+            live[("std", g)] = std
+
+        def normalise_and_store(g):
+            y, sums = live.pop(("y", g))
+            stat_ps = live.pop(("stat", g))
+            std = live.pop(("std", g))
+            rstd = two.tile([P, 1], F32)
+            nc.vector.reciprocal(out=rstd[:], in_=std[:])
+            res = four.tile([P, S * QD], F32)
+            nc.vector.tensor_scalar(
+                out=res[:], in0=y[:], scalar1=stat_ps[:, 0:1], scalar2=rstd[:], op0=ALU.subtract, op1=ALU.mult
+            )
+            nc.sync.dma_start(out=out_view[g], in_=res[:])
+
+        for i in range(GROUPS + 4):
+            if 0 <= i - 4 < GROUPS:
+                deviation(i - 4)
+            if 0 <= i - 2 < GROUPS:
+                product(i - 2)
+            if 0 <= i - 4 < GROUPS:
+                normalise_and_store(i - 4)
+            if i < GROUPS:
+                transpose_and_quantise(i)
+            if 0 <= i - 2 < GROUPS:
+                sum_of_squares(i - 2)
+            if 0 <= i - 1 < GROUPS:
+                multiply(i - 1)
+            if 0 <= i - 3 < GROUPS:
+                sample_statistics(i - 3)

@@ -26,6 +26,7 @@ S = 4
 GROUP_ROWS = P * S
 GROUPS = SAMPLES * L // GROUP_ROWS
 KV_CHUNK = 4
+LOOKAHEAD = 4
 
 FLOPS = 2 * SAMPLES * L * E * QD + 2 * SAMPLES * L * QD * QD
 
@@ -69,24 +70,26 @@ def tile_parallelretention_pb_t_kernel(tc, x, Wq_words, Wq_scales, bq, kv, decay
 
         x_tiles = []
         kv_tiles = []
-        w_words = const.tile([P, PASSES, 2 * QD], U8, align_bytes=64)
-        for g in range(GROUPS):
+
+        def load(g):
             x_sb = x_pool.tile([P, S, E], BF16)
             nc.sync.dma_start(out=x_sb[:], in_=x_view[g])
             x_tiles.append(x_sb)
-            if g == 0:
-                nc.sync.dma_start(
-                    out=w_words[:].bitcast(I32), in_=Wq_words.bitcast(I32).rearrange("c p n -> p c n")
-                )
-                for quad in range(4):
-                    nc.sync.dma_start(
-                        out=w_planes[32 * quad : 32 * quad + 4].bitcast(I32),
-                        in_=Wq_scales.bitcast(I32)[:, 4 * quad : 4 * quad + 4, :].rearrange("c r n -> r c n"),
-                    )
             if g % KV_CHUNK == 0:
                 kv_sb = kv_pool.tile([P, KV_CHUNK, S * QD], BF16)
                 nc.sync.dma_start(out=kv_sb[:], in_=kv_view[:, g : g + KV_CHUNK, :])
                 kv_tiles.append(kv_sb)
+
+        load(0)
+        w_words = const.tile([P, PASSES, 2 * QD], U8, align_bytes=64)
+        nc.sync.dma_start(out=w_words[:].bitcast(I32), in_=Wq_words.bitcast(I32).rearrange("c p n -> p c n"))
+        for quad in range(4):
+            nc.sync.dma_start(
+                out=w_planes[32 * quad : 32 * quad + 4].bitcast(I32),
+                in_=Wq_scales.bitcast(I32)[:, 4 * quad : 4 * quad + 4, :].rearrange("c r n -> r c n"),
+            )
+        for g in range(1, LOOKAHEAD):
+            load(g)
 
         bias = const.tile([P, QD], F32)
         nc.vector.tensor_copy(out=bias[:], in_=bq_bf16[:])
@@ -205,6 +208,8 @@ def tile_parallelretention_pb_t_kernel(tc, x, Wq_words, Wq_scales, bq, kv, decay
             nc.sync.dma_start(out=out_view[g], in_=res[:])
 
         for i in range(GROUPS + 4):
+            if i + LOOKAHEAD < GROUPS:
+                load(i + LOOKAHEAD)
             if 0 <= i - 4 < GROUPS:
                 deviation(i - 4)
             if 0 <= i - 2 < GROUPS:

@@ -98,43 +98,50 @@ def tile_parallelretention_pb_t_kernel(tc, x, Wq_words, Wq_scales, bq, kv, decay
         dT = const.tile([P, QD], BF16)
         nc.vector.tensor_copy(out=dT[:], in_=dT_ps[:, 0, :])
 
+        stat_ps = psum_one.tile([P, GROUPS, 2], F32)
+
         live = {}
 
-        def transpose_and_quantise(g):
+        def start_group(g):
             grouped = two.tile([P, S, PASSES, P, 4], BF16, align_bytes=64)
             codes = two.tile([P, S, PASSES, P], U32, align_bytes=64)
             planes = two.tile([P, S, PASSES, P], U8, align_bytes=64)
-            for j in range(S):
-                xT_ps = psum_x.tile([P, PASSES, 2, P], F32)
-                words = x_tiles[g][:, j, :].bitcast(F32)
-                for c in range(PASSES):
-                    for u in range(2):
-                        nc.tensor.transpose(
-                            xT_ps[:, c, u, :],
-                            words[:, WORDS_PASS * c + u : WORDS_PASS * (c + 1) : 2],
-                            ident_f32[:],
-                        )
-                nc.scalar.copy(out=grouped[:, j].bitcast(F32), in_=xT_ps[:].rearrange("p c u r -> p c r u"))
+            live[("x", g)] = (grouped, codes, planes)
+
+        def transpose_x(g, j):
+            grouped, codes, planes = live[("x", g)]
+            xT_ps = psum_x.tile([P, PASSES, 2, P], F32)
+            words = x_tiles[g][:, j, :].bitcast(F32)
+            for c in range(PASSES):
+                for u in range(2):
+                    nc.tensor.transpose(
+                        xT_ps[:, c, u, :],
+                        words[:, WORDS_PASS * c + u : WORDS_PASS * (c + 1) : 2],
+                        ident_f32[:],
+                    )
+            nc.scalar.copy(out=grouped[:, j].bitcast(F32), in_=xT_ps[:].rearrange("p c u r -> p c r u"))
+
+        def quantise(g, half):
+            grouped, codes, planes = live[("x", g)]
+            blocks = slice(2 * half, 2 * half + 2)
+            nc.vector.quantize_mx(
+                out=codes[:, blocks].rearrange("p j c r -> p (j c r)").bitcast(FP8X4),
+                scales=planes[:, blocks].rearrange("p j c r -> p (j c r)"),
+                in_=grouped[:, blocks].rearrange("p j c r t -> p (j c r t)"),
+            )
+
+        def transpose_kv(g):
             kvT_ps = psum_one.tile([P, S, P], BF16)
             kv_sb = kv_tiles[g // KV_CHUNK]
             for j in range(S):
                 nc.tensor.transpose(kvT_ps[:, j, :], kv_sb[:, g % KV_CHUNK, QD * j : QD * (j + 1)], ident_bf16[:])
-            for half in range(2):
-                blocks = slice(2 * half, 2 * half + 2)
-                if half == 1:
-                    kvT = two.tile([P, S, P], BF16)
-                    nc.vector.tensor_copy(out=kvT[:], in_=kvT_ps[:])
-                nc.vector.quantize_mx(
-                    out=codes[:, blocks].rearrange("p j c r -> p (j c r)").bitcast(FP8X4),
-                    scales=planes[:, blocks].rearrange("p j c r -> p (j c r)"),
-                    in_=grouped[:, blocks].rearrange("p j c r t -> p (j c r t)"),
-                )
-            live[("codes", g)] = (codes, planes, kvT)
+            kvT = two.tile([P, S, P], BF16)
+            nc.vector.tensor_copy(out=kvT[:], in_=kvT_ps[:])
+            live[("kvT", g)] = kvT
 
-        def multiply(g):
-            codes, planes, kvT = live.pop(("codes", g))
+        def project(g):
+            grouped, codes, planes = live.pop(("x", g))
             q_ps = psum_one.tile([P, S, QD], F32)
-            g_ps = psum_one.tile([P, S, QD], F32)
             for j in range(S):
                 for c in range(PASSES):
                     nc.tensor.matmul_mx(
@@ -146,16 +153,26 @@ def tile_parallelretention_pb_t_kernel(tc, x, Wq_words, Wq_scales, bq, kv, decay
                         start=(c == 0),
                         stop=(c == PASSES - 1),
                     )
-            for j in range(S):
-                nc.tensor.matmul(out=g_ps[:, j, :], lhsT=kvT[:, j, :], rhs=dT[:], start=True, stop=True)
-            live[("qg", g)] = (q_ps, g_ps)
+            live[("q", g)] = q_ps
 
-        def product(g):
-            q_ps, g_ps = live.pop(("qg", g))
+        def add_bias(g):
+            q_ps = live.pop(("q", g))
             biased = two.tile([P, S, QD], F32)
             nc.vector.tensor_tensor(
                 out=biased[:], in0=q_ps[:], in1=bias[:].unsqueeze(1).to_broadcast([P, S, QD]), op=ALU.add
             )
+            live[("biased", g)] = biased
+
+        def decay(g):
+            kvT = live.pop(("kvT", g))
+            g_ps = psum_one.tile([P, S, QD], F32)
+            for j in range(S):
+                nc.tensor.matmul(out=g_ps[:, j, :], lhsT=kvT[:, j, :], rhs=dT[:], start=True, stop=True)
+            live[("g", g)] = g_ps
+
+        def product(g):
+            g_ps = live.pop(("g", g))
+            biased = live.pop(("biased", g))
             y = four.tile([P, S * QD], F32)
             sums = four.tile([P, 2, 8], F32)
             nc.vector.scalar_tensor_tensor(
@@ -176,51 +193,69 @@ def tile_parallelretention_pb_t_kernel(tc, x, Wq_words, Wq_scales, bq, kv, decay
 
         def sample_statistics(g):
             y, sums = live[("y", g)]
-            stat_ps = psum_one.tile([P, 2], F32)
-            nc.tensor.matmul(out=stat_ps[:], lhsT=sample_mean[:], rhs=sums[:, :, 0], start=True, stop=True)
-            live[("stat", g)] = stat_ps
+            nc.tensor.matmul(out=stat_ps[:, g, :], lhsT=sample_mean[:], rhs=sums[:, :, 0], start=True, stop=True)
 
-        def deviation(g):
-            stat_ps = live[("stat", g)]
+        def minus_variance(g):
             minus_var = two.tile([P, 1], F32)
             nc.vector.tensor_scalar(
                 out=minus_var[:],
-                in0=stat_ps[:, 0:1],
-                scalar1=stat_ps[:, 0:1],
-                scalar2=stat_ps[:, 1:2],
+                in0=stat_ps[:, g, 0:1],
+                scalar1=stat_ps[:, g, 0:1],
+                scalar2=stat_ps[:, g, 1:2],
                 op0=ALU.mult,
                 op1=ALU.subtract,
             )
+            live[("minus_var", g)] = minus_var
+
+        def deviation(g):
+            minus_var = live.pop(("minus_var", g))
             std = two.tile([P, 1], F32)
             nc.scalar.activation(out=std[:], in_=minus_var[:], func=ACT.Sqrt, bias=eps[:], scale=-1.0)
             live[("std", g)] = std
 
         def normalise_and_store(g):
             y, sums = live.pop(("y", g))
-            stat_ps = live.pop(("stat", g))
             std = live.pop(("std", g))
             rstd = two.tile([P, 1], F32)
             nc.vector.reciprocal(out=rstd[:], in_=std[:])
             res = four.tile([P, S * QD], F32)
             nc.vector.tensor_scalar(
-                out=res[:], in0=y[:], scalar1=stat_ps[:, 0:1], scalar2=rstd[:], op0=ALU.subtract, op1=ALU.mult
+                out=res[:], in0=y[:], scalar1=stat_ps[:, g, 0:1], scalar2=rstd[:], op0=ALU.subtract, op1=ALU.mult
             )
             nc.sync.dma_start(out=out_view[g], in_=res[:])
 
-        for i in range(GROUPS + 4):
-            if i + LOOKAHEAD < GROUPS:
+        def in_range(g):
+            return 0 <= g < GROUPS
+
+        for i in range(GROUPS + 5):
+            if in_range(i + LOOKAHEAD):
                 load(i + LOOKAHEAD)
-            if 0 <= i - 4 < GROUPS:
-                deviation(i - 4)
-            if 0 <= i - 2 < GROUPS:
+            if in_range(i - 4):
+                minus_variance(i - 4)
+            if in_range(i - 2):
                 product(i - 2)
-            if 0 <= i - 4 < GROUPS:
-                normalise_and_store(i - 4)
-            if i < GROUPS:
-                transpose_and_quantise(i)
-            if 0 <= i - 2 < GROUPS:
+            if in_range(i - 5):
+                normalise_and_store(i - 5)
+            if in_range(i):
+                start_group(i)
+                transpose_x(i, 0)
+                transpose_x(i, 1)
+            if in_range(i - 1):
+                project(i - 1)
+            if in_range(i - 4):
+                deviation(i - 4)
+            if in_range(i - 2):
                 sum_of_squares(i - 2)
-            if 0 <= i - 1 < GROUPS:
-                multiply(i - 1)
-            if 0 <= i - 3 < GROUPS:
+            if in_range(i):
+                quantise(i, 0)
+            if in_range(i - 1):
+                add_bias(i - 1)
+            if in_range(i):
+                transpose_x(i, 2)
+                transpose_x(i, 3)
+                transpose_kv(i)
+                quantise(i, 1)
+            if in_range(i - 1):
+                decay(i - 1)
+            if in_range(i - 3):
                 sample_statistics(i - 3)

@@ -25,7 +25,6 @@ WORDS_PASS = K_PASS // 2
 S = 4
 GROUP_ROWS = P * S
 GROUPS = SAMPLES * L // GROUP_ROWS
-KV_CHUNK = 4
 LOOKAHEAD = 4
 
 FLOPS = 2 * SAMPLES * L * E * QD + 2 * SAMPLES * L * QD * QD
@@ -34,18 +33,23 @@ FLOPS = 2 * SAMPLES * L * E * QD + 2 * SAMPLES * L * QD * QD
 def tile_parallelretention_pb_t_kernel(tc, x, Wq_words, Wq_scales, bq, kv, decay_mask, out):
     nc = tc.nc
     x_view = x.rearrange("b h l e -> (b h l) e").rearrange("(g p j) e -> g p j e", p=P, j=S)
-    kv_view = kv.rearrange("b h l k -> (b h l) k").rearrange("(g p j) k -> p g (j k)", p=P, j=S)
+    kv_view = kv.rearrange("b h l k -> (b h l) k").rearrange("(g p j) k -> g p j k", p=P, j=S)
     out_view = out.rearrange("b l q -> (b l) q").rearrange("(g p j) q -> g p (j q)", p=P, j=S)
 
     with ExitStack() as ctx:
         ctx.enter_context(tc.manual_schedule())
         const = ctx.enter_context(tc.tile_pool(name="const", bufs=1))
         x_pool = ctx.enter_context(tc.tile_pool(name="x_pool", bufs=GROUPS))
-        kv_pool = ctx.enter_context(tc.tile_pool(name="kv_pool", bufs=GROUPS // KV_CHUNK))
+        kv_pool = ctx.enter_context(tc.tile_pool(name="kv_pool", bufs=GROUPS))
         two = ctx.enter_context(tc.tile_pool(name="two", bufs=2))
         four = ctx.enter_context(tc.tile_pool(name="four", bufs=4))
         psum_x = ctx.enter_context(tc.psum_pool(name="psum_x", bufs=S))
         psum_one = ctx.enter_context(tc.psum_pool(name="psum_one", bufs=1))
+
+        d_sb = const.tile([P, P], BF16)
+        nc.scalar.dma_start(out=d_sb[:], in_=decay_mask.rearrange("o q k -> (o q) k"))
+        bq_bf16 = const.tile([P, QD], BF16)
+        nc.scalar.dma_start(out=bq_bf16[:], in_=bq.partition_broadcast(P))
 
         w_planes = const.tile([P, PASSES, QD], U8, align_bytes=64)
         nc.vector.memset(w_planes[:].bitcast(I32), 0)
@@ -56,29 +60,25 @@ def tile_parallelretention_pb_t_kernel(tc, x, Wq_words, Wq_scales, bq, kv, decay
         for a in range(P // 32):
             rows = slice(32 * a, 32 * a + 32)
             nc.vector.memset(sample_mean[rows, rows], 1.0 / (L * QD))
-        warm = const.tile([P, 1], F32)
-        nc.scalar.activation(out=warm[:], in_=eps[:], func=ACT.Sqrt)
         ident_f32 = const.tile([P, P], F32)
         make_identity(nc, ident_f32[:])
         ident_bf16 = const.tile([P, P], BF16)
         make_identity(nc, ident_bf16[:])
 
-        d_sb = const.tile([P, P], BF16)
-        nc.scalar.dma_start(out=d_sb[:], in_=decay_mask.rearrange("o q k -> (o q) k"))
-        bq_bf16 = const.tile([P, QD], BF16)
-        nc.scalar.dma_start(out=bq_bf16[:], in_=bq.partition_broadcast(P))
+        warm = const.tile([P, 1], F32)
+        nc.scalar.activation(out=warm[:], in_=eps[:], func=ACT.Abs_reciprocal_sqrt)
 
         x_tiles = []
         kv_tiles = []
 
         def load(g):
             x_sb = x_pool.tile([P, S, E], BF16)
-            nc.sync.dma_start(out=x_sb[:], in_=x_view[g])
+            for j in range(S):
+                nc.sync.dma_start(out=x_sb[:, j, :], in_=x_view[g, :, j, :])
             x_tiles.append(x_sb)
-            if g % KV_CHUNK == 0:
-                kv_sb = kv_pool.tile([P, KV_CHUNK, S * QD], BF16)
-                nc.sync.dma_start(out=kv_sb[:], in_=kv_view[:, g : g + KV_CHUNK, :])
-                kv_tiles.append(kv_sb)
+            kv_sb = kv_pool.tile([P, S, QD], BF16)
+            nc.sync.dma_start(out=kv_sb[:], in_=kv_view[g])
+            kv_tiles.append(kv_sb)
 
         load(0)
         w_words = const.tile([P, PASSES, 2 * QD], U8, align_bytes=64)
@@ -132,9 +132,8 @@ def tile_parallelretention_pb_t_kernel(tc, x, Wq_words, Wq_scales, bq, kv, decay
 
         def transpose_kv(g):
             kvT_ps = psum_one.tile([P, S, P], BF16)
-            kv_sb = kv_tiles[g // KV_CHUNK]
             for j in range(S):
-                nc.tensor.transpose(kvT_ps[:, j, :], kv_sb[:, g % KV_CHUNK, QD * j : QD * (j + 1)], ident_bf16[:])
+                nc.tensor.transpose(kvT_ps[:, j, :], kv_tiles[g][:, j, :], ident_bf16[:])
             kvT = two.tile([P, S, P], BF16)
             nc.vector.tensor_copy(out=kvT[:], in_=kvT_ps[:])
             live[("kvT", g)] = kvT
@@ -207,17 +206,17 @@ def tile_parallelretention_pb_t_kernel(tc, x, Wq_words, Wq_scales, bq, kv, decay
             )
             live[("minus_var", g)] = minus_var
 
-        def deviation(g):
+        def inverse_deviation(g):
             minus_var = live.pop(("minus_var", g))
-            std = two.tile([P, 1], F32)
-            nc.scalar.activation(out=std[:], in_=minus_var[:], func=ACT.Sqrt, bias=eps[:], scale=-1.0)
-            live[("std", g)] = std
+            rstd = two.tile([P, 1], F32)
+            nc.scalar.activation(
+                out=rstd[:], in_=minus_var[:], func=ACT.Abs_reciprocal_sqrt, bias=eps[:], scale=-1.0
+            )
+            live[("rstd", g)] = rstd
 
         def normalise_and_store(g):
             y, sums = live.pop(("y", g))
-            std = live.pop(("std", g))
-            rstd = two.tile([P, 1], F32)
-            nc.vector.reciprocal(out=rstd[:], in_=std[:])
+            rstd = live.pop(("rstd", g))
             res = four.tile([P, S * QD], F32)
             nc.vector.tensor_scalar(
                 out=res[:], in0=y[:], scalar1=stat_ps[:, g, 0:1], scalar2=rstd[:], op0=ALU.subtract, op1=ALU.mult
@@ -227,27 +226,27 @@ def tile_parallelretention_pb_t_kernel(tc, x, Wq_words, Wq_scales, bq, kv, decay
         def in_range(g):
             return 0 <= g < GROUPS
 
-        for i in range(GROUPS + 5):
+        for i in range(GROUPS + 3):
             if in_range(i + LOOKAHEAD):
                 load(i + LOOKAHEAD)
-            if in_range(i - 4):
-                minus_variance(i - 4)
+            if in_range(i - 3):
+                minus_variance(i - 3)
             if in_range(i - 2):
                 product(i - 2)
-            if in_range(i - 5):
-                normalise_and_store(i - 5)
             if in_range(i):
                 start_group(i)
                 transpose_x(i, 0)
                 transpose_x(i, 1)
             if in_range(i - 1):
                 project(i - 1)
-            if in_range(i - 4):
-                deviation(i - 4)
+            if in_range(i - 3):
+                inverse_deviation(i - 3)
             if in_range(i - 2):
                 sum_of_squares(i - 2)
             if in_range(i):
                 quantise(i, 0)
+            if in_range(i - 3):
+                normalise_and_store(i - 3)
             if in_range(i - 1):
                 add_bias(i - 1)
             if in_range(i):
@@ -257,5 +256,5 @@ def tile_parallelretention_pb_t_kernel(tc, x, Wq_words, Wq_scales, bq, kv, decay
                 quantise(i, 1)
             if in_range(i - 1):
                 decay(i - 1)
-            if in_range(i - 3):
-                sample_statistics(i - 3)
+            if in_range(i - 2):
+                sample_statistics(i - 2)

@@ -134,6 +134,10 @@ def tile_parallelretention_pb_t_kernel(tc, x, Wq_words, Wq_scales, bq, kv, decay
             kvT_ps = psum_one.tile([P, S, P], BF16)
             for j in range(S):
                 nc.tensor.transpose(kvT_ps[:, j, :], kv_tiles[g][:, j, :], ident_bf16[:])
+            live[("kvT_ps", g)] = kvT_ps
+
+        def copy_kv(g):
+            kvT_ps = live.pop(("kvT_ps", g))
             kvT = two.tile([P, S, P], BF16)
             nc.vector.tensor_copy(out=kvT[:], in_=kvT_ps[:])
             live[("kvT", g)] = kvT
@@ -226,35 +230,37 @@ def tile_parallelretention_pb_t_kernel(tc, x, Wq_words, Wq_scales, bq, kv, decay
         def in_range(g):
             return 0 <= g < GROUPS
 
-        for i in range(GROUPS + 3):
+        for i in range(GROUPS + 4):
             if in_range(i + LOOKAHEAD):
                 load(i + LOOKAHEAD)
-            if in_range(i - 3):
-                minus_variance(i - 3)
-            if in_range(i - 2):
-                product(i - 2)
             if in_range(i):
                 start_group(i)
                 transpose_x(i, 0)
                 transpose_x(i, 1)
+            if in_range(i - 4):
+                normalise_and_store(i - 4)
             if in_range(i - 1):
-                project(i - 1)
-            if in_range(i - 3):
-                inverse_deviation(i - 3)
+                quantise(i - 1, 1)
             if in_range(i - 2):
-                sum_of_squares(i - 2)
-            if in_range(i):
-                quantise(i, 0)
-            if in_range(i - 3):
-                normalise_and_store(i - 3)
+                add_bias(i - 2)
             if in_range(i - 1):
-                add_bias(i - 1)
+                copy_kv(i - 1)
+            if in_range(i - 2):
+                product(i - 2)
+            if in_range(i - 3):
+                sample_statistics(i - 3)
             if in_range(i):
                 transpose_x(i, 2)
                 transpose_x(i, 3)
                 transpose_kv(i)
-                quantise(i, 1)
-            if in_range(i - 1):
-                decay(i - 1)
+            if in_range(i - 3):
+                minus_variance(i - 3)
+            if in_range(i):
+                quantise(i, 0)
+            if in_range(i - 3):
+                inverse_deviation(i - 3)
             if in_range(i - 2):
-                sample_statistics(i - 2)
+                sum_of_squares(i - 2)
+            if in_range(i - 1):
+                project(i - 1)
+                decay(i - 1)

@@ -45,6 +45,7 @@ def tile_parallelretention_pb_t_kernel(tc, x, Wq_words, Wq_scales, bq, kv, decay
         four = ctx.enter_context(tc.tile_pool(name="four", bufs=4))
         psum_x = ctx.enter_context(tc.psum_pool(name="psum_x", bufs=S))
         psum_one = ctx.enter_context(tc.psum_pool(name="psum_one", bufs=1))
+        psum_half = ctx.enter_context(tc.psum_pool(name="psum_half", bufs=2))
 
         d_sb = const.tile([P, P], BF16)
         nc.scalar.dma_start(out=d_sb[:], in_=decay_mask.rearrange("o q k -> (o q) k"))
@@ -98,7 +99,7 @@ def tile_parallelretention_pb_t_kernel(tc, x, Wq_words, Wq_scales, bq, kv, decay
         dT = const.tile([P, QD], BF16)
         nc.vector.tensor_copy(out=dT[:], in_=dT_ps[:, 0, :])
 
-        stat_ps = psum_one.tile([P, GROUPS, 2], F32)
+        stat_ps = psum_one.tile([P, GROUPS, 4], F32)
 
         live = {}
 
@@ -134,21 +135,19 @@ def tile_parallelretention_pb_t_kernel(tc, x, Wq_words, Wq_scales, bq, kv, decay
             kvT_ps = psum_one.tile([P, S, P], BF16)
             for j in range(S):
                 nc.tensor.transpose(kvT_ps[:, j, :], kv_tiles[g][:, j, :], ident_bf16[:])
-            live[("kvT_ps", g)] = kvT_ps
-
-        def copy_kv(g):
-            kvT_ps = live.pop(("kvT_ps", g))
             kvT = two.tile([P, S, P], BF16)
-            nc.vector.tensor_copy(out=kvT[:], in_=kvT_ps[:])
+            nc.scalar.copy(out=kvT[:], in_=kvT_ps[:])
             live[("kvT", g)] = kvT
 
-        def project(g):
-            grouped, codes, planes = live.pop(("x", g))
-            q_ps = psum_one.tile([P, S, QD], F32)
-            for j in range(S):
+        def multiply(g, half):
+            grouped, codes, planes = live[("x", g)]
+            kvT = live[("kvT", g)]
+            qg_ps = psum_half.tile([P, 2, 2, QD], F32)
+            for b in range(2):
+                j = 2 * half + b
                 for c in range(PASSES):
                     nc.tensor.matmul_mx(
-                        out=q_ps[:, j, :],
+                        out=qg_ps[:, 0, b, :],
                         lhsT=codes[:, j, c, :].bitcast(FP8X4),
                         lhsT_scale=planes[:, j, c, :],
                         rhs=w_words[:, c, :].bitcast(FP4X4),
@@ -156,55 +155,64 @@ def tile_parallelretention_pb_t_kernel(tc, x, Wq_words, Wq_scales, bq, kv, decay
                         start=(c == 0),
                         stop=(c == PASSES - 1),
                     )
-            live[("q", g)] = q_ps
+            for b in range(2):
+                nc.tensor.matmul(out=qg_ps[:, 1, b, :], lhsT=kvT[:, 2 * half + b, :], rhs=dT[:], start=True, stop=True)
+            live[("qg", g, half)] = qg_ps
 
-        def add_bias(g):
-            q_ps = live.pop(("q", g))
-            biased = two.tile([P, S, QD], F32)
+        def add_bias(g, half):
+            qg_ps = live[("qg", g, half)]
+            if half == 0:
+                biased = two.tile([P, 2, 2, QD], F32)
+                live[("biased", g)] = biased
+            biased = live[("biased", g)]
             nc.vector.tensor_tensor(
-                out=biased[:], in0=q_ps[:], in1=bias[:].unsqueeze(1).to_broadcast([P, S, QD]), op=ALU.add
+                out=biased[:, half], in0=qg_ps[:, 0], in1=bias[:].unsqueeze(1).to_broadcast([P, 2, QD]), op=ALU.add
             )
-            live[("biased", g)] = biased
 
-        def decay(g):
-            kvT = live.pop(("kvT", g))
-            g_ps = psum_one.tile([P, S, QD], F32)
-            for j in range(S):
-                nc.tensor.matmul(out=g_ps[:, j, :], lhsT=kvT[:, j, :], rhs=dT[:], start=True, stop=True)
-            live[("g", g)] = g_ps
-
-        def product(g):
-            g_ps = live.pop(("g", g))
-            biased = live.pop(("biased", g))
-            y = four.tile([P, S * QD], F32)
-            sums = four.tile([P, 2, 8], F32)
+        def product(g, half):
+            qg_ps = live.pop(("qg", g, half))
+            biased = live[("biased", g)]
+            if half == 0:
+                y = four.tile([P, 2, 2 * QD], F32)
+                sums = four.tile([P, 3, 8], F32)
+                live[("y", g)] = (y, sums)
+            y, sums = live[("y", g)]
             nc.vector.scalar_tensor_tensor(
-                out=y[:],
-                in0=g_ps[:].rearrange("p j q -> p (j q)"),
+                out=y[:, half, :],
+                in0=qg_ps[:, 1].rearrange("p b q -> p (b q)"),
                 scalar=1.0,
-                in1=biased[:].rearrange("p j q -> p (j q)"),
+                in1=biased[:, half].rearrange("p b q -> p (b q)"),
                 op0=ALU.mult,
                 op1=ALU.mult,
-                accum_out=sums[:, 0, 0:1],
+                accum_out=sums[:, half, 0:1],
             )
-            live[("y", g)] = (y, sums)
 
         def sum_of_squares(g):
             y, sums = live[("y", g)]
             squares = two.tile([P, S * QD], F32)
-            nc.scalar.activation(out=squares[:], in_=y[:], func=ACT.Square, accum_out=sums[:, 1, 0:1])
+            nc.scalar.activation(
+                out=squares[:], in_=y[:].rearrange("p h n -> p (h n)"), func=ACT.Square, accum_out=sums[:, 2, 0:1]
+            )
 
         def sample_statistics(g):
             y, sums = live[("y", g)]
-            nc.tensor.matmul(out=stat_ps[:, g, :], lhsT=sample_mean[:], rhs=sums[:, :, 0], start=True, stop=True)
+            nc.tensor.matmul(out=stat_ps[:, g, 0:3], lhsT=sample_mean[:], rhs=sums[:, :, 0], start=True, stop=True)
+
+        def mean_of_sample(g):
+            mean = two.tile([P, 1], F32)
+            nc.vector.tensor_scalar(
+                out=mean[:], in0=stat_ps[:, g, 0:1], scalar1=stat_ps[:, g, 1:2], scalar2=1.0, op0=ALU.add, op1=ALU.mult
+            )
+            live[("mean", g)] = mean
 
         def minus_variance(g):
+            mean = live[("mean", g)]
             minus_var = two.tile([P, 1], F32)
             nc.vector.tensor_scalar(
                 out=minus_var[:],
-                in0=stat_ps[:, g, 0:1],
-                scalar1=stat_ps[:, g, 0:1],
-                scalar2=stat_ps[:, g, 1:2],
+                in0=mean[:],
+                scalar1=mean[:],
+                scalar2=stat_ps[:, g, 2:3],
                 op0=ALU.mult,
                 op1=ALU.subtract,
             )
@@ -221,9 +229,15 @@ def tile_parallelretention_pb_t_kernel(tc, x, Wq_words, Wq_scales, bq, kv, decay
         def normalise_and_store(g):
             y, sums = live.pop(("y", g))
             rstd = live.pop(("rstd", g))
+            mean = live.pop(("mean", g))
             res = four.tile([P, S * QD], F32)
             nc.vector.tensor_scalar(
-                out=res[:], in0=y[:], scalar1=stat_ps[:, g, 0:1], scalar2=rstd[:], op0=ALU.subtract, op1=ALU.mult
+                out=res[:],
+                in0=y[:].rearrange("p h n -> p (h n)"),
+                scalar1=mean[:],
+                scalar2=rstd[:],
+                op0=ALU.subtract,
+                op1=ALU.mult,
             )
             nc.sync.dma_start(out=out_view[g], in_=res[:])
 
@@ -237,30 +251,35 @@ def tile_parallelretention_pb_t_kernel(tc, x, Wq_words, Wq_scales, bq, kv, decay
                 start_group(i)
                 transpose_x(i, 0)
                 transpose_x(i, 1)
-            if in_range(i - 4):
-                normalise_and_store(i - 4)
             if in_range(i - 1):
                 quantise(i - 1, 1)
             if in_range(i - 2):
-                add_bias(i - 2)
-            if in_range(i - 1):
-                copy_kv(i - 1)
+                add_bias(i - 2, 1)
+            if in_range(i - 4):
+                normalise_and_store(i - 4)
             if in_range(i - 2):
-                product(i - 2)
+                product(i - 2, 1)
+            if in_range(i - 1):
+                multiply(i - 1, 0)
             if in_range(i - 3):
                 sample_statistics(i - 3)
             if in_range(i):
                 transpose_x(i, 2)
                 transpose_x(i, 3)
                 transpose_kv(i)
+            if in_range(i - 1):
+                add_bias(i - 1, 0)
             if in_range(i - 3):
-                minus_variance(i - 3)
+                mean_of_sample(i - 3)
             if in_range(i):
                 quantise(i, 0)
+            if in_range(i - 3):
+                minus_variance(i - 3)
+            if in_range(i - 1):
+                product(i - 1, 0)
             if in_range(i - 3):
                 inverse_deviation(i - 3)
             if in_range(i - 2):
                 sum_of_squares(i - 2)
             if in_range(i - 1):
-                project(i - 1)
-                decay(i - 1)
+                multiply(i - 1, 1)

@@ -49,8 +49,11 @@ def tile_parallelretention_pb_t_kernel(tc, x, Wq_words, Wq_scales, bq, kv, decay
 
         d_sb = const.tile([P, P], BF16)
         nc.scalar.dma_start(out=d_sb[:], in_=decay_mask.rearrange("o q k -> (o q) k"))
-        bq_bf16 = const.tile([P, QD], BF16)
-        nc.scalar.dma_start(out=bq_bf16[:], in_=bq.partition_broadcast(P))
+        bq_row = const.tile([P, QD], BF16)
+        nc.gpsimd.memset(bq_row[:], 0.0)
+        nc.scalar.dma_start(out=bq_row[0:1, :], in_=bq.rearrange("(o q) -> o q", o=1))
+        ones = const.tile([P, P], BF16)
+        nc.gpsimd.memset(ones[:], 1.0)
 
         w_planes = const.tile([P, PASSES, QD], U8, align_bytes=64)
         nc.vector.memset(w_planes[:].bitcast(I32), 0)
@@ -92,12 +95,14 @@ def tile_parallelretention_pb_t_kernel(tc, x, Wq_words, Wq_scales, bq, kv, decay
         for g in range(1, LOOKAHEAD):
             load(g)
 
-        bias = const.tile([P, QD], F32)
-        nc.vector.tensor_copy(out=bias[:], in_=bq_bf16[:])
         dT_ps = psum_one.tile([P, S, P], BF16, name="kvT_ps")
         nc.tensor.transpose(dT_ps[:, 0, :], d_sb[:], ident_bf16[:])
         dT = const.tile([P, QD], BF16)
         nc.vector.tensor_copy(out=dT[:], in_=dT_ps[:, 0, :])
+        bias_ps = psum_half.tile([P, 2, 2, QD], F32, name="qg_ps")
+        nc.tensor.matmul(out=bias_ps[:, 0, 0, :], lhsT=ones[:], rhs=bq_row[:], start=True, stop=True)
+        bias = const.tile([P, QD], F32)
+        nc.vector.tensor_copy(out=bias[:], in_=bias_ps[:, 0, 0, :])
 
         stat_ps = psum_one.tile([P, GROUPS, 4], F32)
 

@@ -25,6 +25,7 @@ WORDS_PASS = K_PASS // 2
 S = 4
 GROUP_ROWS = P * S
 GROUPS = SAMPLES * L // GROUP_ROWS
+LAST = GROUPS - 1
 LOOKAHEAD = 4
 
 FLOPS = 2 * SAMPLES * L * E * QD + 2 * SAMPLES * L * QD * QD
@@ -35,6 +36,10 @@ def tile_parallelretention_pb_t_kernel(tc, x, Wq_words, Wq_scales, bq, kv, decay
     x_view = x.rearrange("b h l e -> (b h l) e").rearrange("(g p j) e -> g p j e", p=P, j=S)
     kv_view = kv.rearrange("b h l k -> (b h l) k").rearrange("(g p j) k -> g p j k", p=P, j=S)
     out_view = out.rearrange("b l q -> (b l) q").rearrange("(g p j) q -> g p (j q)", p=P, j=S)
+    first_row = LAST * GROUP_ROWS
+    x_last = x.rearrange("b h l e -> (b h l) e")[first_row:, :].rearrange("(h p j) e -> p h j e", p=P, j=2)
+    kv_last = kv.rearrange("b h l k -> (b h l) k")[first_row:, :].rearrange("(h p j) k -> p h (j k)", p=P, j=2)
+    out_last = out.rearrange("b l q -> (b l) q")[first_row:, :].rearrange("(h p j) q -> h p (j q)", p=P, j=2)
 
     with ExitStack() as ctx:
         ctx.enter_context(tc.manual_schedule())
@@ -64,6 +69,11 @@ def tile_parallelretention_pb_t_kernel(tc, x, Wq_words, Wq_scales, bq, kv, decay
         for a in range(P // 32):
             rows = slice(32 * a, 32 * a + 32)
             nc.vector.memset(sample_mean[rows, rows], 1.0 / (L * QD))
+        half_mean = const.tile([P, P], F32)
+        nc.vector.memset(half_mean[:], 0.0)
+        for a in range(2):
+            rows = slice(64 * a, 64 * a + 64)
+            nc.vector.memset(half_mean[rows, rows], 1.0 / (L * QD))
         ident_f32 = const.tile([P, P], F32)
         make_identity(nc, ident_f32[:])
         ident_bf16 = const.tile([P, P], BF16)
@@ -78,10 +88,14 @@ def tile_parallelretention_pb_t_kernel(tc, x, Wq_words, Wq_scales, bq, kv, decay
         def load(g):
             x_sb = x_pool.tile([P, S, E], BF16)
             for j in range(S):
-                nc.sync.dma_start(out=x_sb[:, j, :], in_=x_view[g, :, j, :])
+                rows = x_view[g, :, j, :] if g < LAST else x_last[:, j // 2, j % 2, :]
+                nc.sync.dma_start(out=x_sb[:, j, :], in_=rows)
             x_tiles.append(x_sb)
             kv_sb = kv_pool.tile([P, S, QD], BF16)
-            nc.sync.dma_start(out=kv_sb[:], in_=kv_view[g])
+            if g < LAST:
+                nc.sync.dma_start(out=kv_sb[:], in_=kv_view[g])
+            else:
+                nc.sync.dma_start(out=kv_sb[:].rearrange("p (h j) k -> p h (j k)", h=2), in_=kv_last)
             kv_tiles.append(kv_sb)
 
         load(0)
@@ -104,7 +118,7 @@ def tile_parallelretention_pb_t_kernel(tc, x, Wq_words, Wq_scales, bq, kv, decay
         bias = const.tile([P, QD], F32)
         nc.vector.tensor_copy(out=bias[:], in_=bias_ps[:, 0, 0, :])
 
-        stat_ps = psum_one.tile([P, GROUPS, 4], F32)
+        stat_ps = psum_one.tile([P, GROUPS + 1, 4], F32)
 
         live = {}
 
@@ -140,14 +154,24 @@ def tile_parallelretention_pb_t_kernel(tc, x, Wq_words, Wq_scales, bq, kv, decay
             kvT_ps = psum_one.tile([P, S, P], BF16)
             for j in range(S):
                 nc.tensor.transpose(kvT_ps[:, j, :], kv_tiles[g][:, j, :], ident_bf16[:])
+            live[("kvT_ps", g)] = kvT_ps
+
+        def copy_kv(g):
+            kvT_ps = live.pop(("kvT_ps", g))
             kvT = two.tile([P, S, P], BF16)
-            nc.scalar.copy(out=kvT[:], in_=kvT_ps[:])
+            if g % 2 == 0:
+                nc.vector.tensor_copy(out=kvT[:], in_=kvT_ps[:])
+            else:
+                nc.scalar.copy(out=kvT[:], in_=kvT_ps[:])
             live[("kvT", g)] = kvT
 
         def multiply(g, half):
             grouped, codes, planes = live[("x", g)]
             kvT = live[("kvT", g)]
-            qg_ps = psum_half.tile([P, 2, 2, QD], F32)
+            if g == LAST and half == 1:
+                qg_ps = psum_x.tile([P, 2, 2, QD], F32, name="xT_ps")
+            else:
+                qg_ps = psum_half.tile([P, 2, 2, QD], F32)
             for b in range(2):
                 j = 2 * half + b
                 for c in range(PASSES):
@@ -179,7 +203,7 @@ def tile_parallelretention_pb_t_kernel(tc, x, Wq_words, Wq_scales, bq, kv, decay
             biased = live[("biased", g)]
             if half == 0:
                 y = four.tile([P, 2, 2 * QD], F32)
-                sums = four.tile([P, 3, 8], F32)
+                sums = four.tile([P, 4, 8], F32)
                 live[("y", g)] = (y, sums)
             y, sums = live[("y", g)]
             nc.vector.scalar_tensor_tensor(
@@ -192,99 +216,146 @@ def tile_parallelretention_pb_t_kernel(tc, x, Wq_words, Wq_scales, bq, kv, decay
                 accum_out=sums[:, half, 0:1],
             )
 
-        def sum_of_squares(g):
+        def sum_of_squares(g, part=None):
             y, sums = live[("y", g)]
-            squares = two.tile([P, S * QD], F32)
-            nc.scalar.activation(
-                out=squares[:], in_=y[:].rearrange("p h n -> p (h n)"), func=ACT.Square, accum_out=sums[:, 2, 0:1]
-            )
+            if part is None:
+                squares = two.tile([P, S * QD], F32)
+                nc.scalar.activation(
+                    out=squares[:], in_=y[:].rearrange("p h n -> p (h n)"), func=ACT.Square, accum_out=sums[:, 2, 0:1]
+                )
+            else:
+                squares = two.tile([P, 2 * QD], F32)
+                nc.scalar.activation(
+                    out=squares[:], in_=y[:, part, :], func=ACT.Square, accum_out=sums[:, 2 + part, 0:1]
+                )
 
-        def sample_statistics(g):
+        def sample_statistics(g, part=None):
             y, sums = live[("y", g)]
-            nc.tensor.matmul(out=stat_ps[:, g, 0:3], lhsT=sample_mean[:], rhs=sums[:, :, 0], start=True, stop=True)
+            if part is None:
+                nc.tensor.matmul(out=stat_ps[:, g, 0:3], lhsT=sample_mean[:], rhs=sums[:, 0:3, 0], start=True, stop=True)
+            else:
+                nc.tensor.matmul(
+                    out=stat_ps[:, g + part, 0:2], lhsT=half_mean[:], rhs=sums[:, part:4:2, 0], start=True, stop=True
+                )
 
-        def mean_of_sample(g):
-            mean = two.tile([P, 1], F32)
+        def mean_of_sample(g, part=None):
+            if part is None:
+                mean = four.tile([P, 1], F32)
+                nc.vector.tensor_scalar(
+                    out=mean[:],
+                    in0=stat_ps[:, g, 0:1],
+                    scalar1=stat_ps[:, g, 1:2],
+                    scalar2=1.0,
+                    op0=ALU.add,
+                    op1=ALU.mult,
+                )
+                live[("mean", g, part)] = mean[:]
+            else:
+                live[("mean", g, part)] = stat_ps[:, g + part, 0:1]
+
+        def minus_variance(g, part=None):
+            mean = live[("mean", g, part)]
+            mean_square = stat_ps[:, g, 2:3] if part is None else stat_ps[:, g + part, 1:2]
+            minus_var = four.tile([P, 1], F32)
             nc.vector.tensor_scalar(
-                out=mean[:], in0=stat_ps[:, g, 0:1], scalar1=stat_ps[:, g, 1:2], scalar2=1.0, op0=ALU.add, op1=ALU.mult
+                out=minus_var[:], in0=mean, scalar1=mean, scalar2=mean_square, op0=ALU.mult, op1=ALU.subtract
             )
-            live[("mean", g)] = mean
+            live[("minus_var", g, part)] = minus_var
 
-        def minus_variance(g):
-            mean = live[("mean", g)]
-            minus_var = two.tile([P, 1], F32)
-            nc.vector.tensor_scalar(
-                out=minus_var[:],
-                in0=mean[:],
-                scalar1=mean[:],
-                scalar2=stat_ps[:, g, 2:3],
-                op0=ALU.mult,
-                op1=ALU.subtract,
-            )
-            live[("minus_var", g)] = minus_var
-
-        def inverse_deviation(g):
-            minus_var = live.pop(("minus_var", g))
-            rstd = two.tile([P, 1], F32)
+        def inverse_deviation(g, part=None):
+            minus_var = live.pop(("minus_var", g, part))
+            rstd = four.tile([P, 1], F32)
             nc.scalar.activation(
                 out=rstd[:], in_=minus_var[:], func=ACT.Abs_reciprocal_sqrt, bias=eps[:], scale=-1.0
             )
-            live[("rstd", g)] = rstd
+            live[("rstd", g, part)] = rstd
 
-        def normalise_and_store(g):
-            y, sums = live.pop(("y", g))
-            rstd = live.pop(("rstd", g))
-            mean = live.pop(("mean", g))
-            res = four.tile([P, S * QD], F32)
+        def normalise_and_store(g, part=None):
+            y, sums = live[("y", g)]
+            rstd = live.pop(("rstd", g, part))
+            mean = live.pop(("mean", g, part))
+            if part is None:
+                res = four.tile([P, S * QD], F32)
+                values, rows = y[:].rearrange("p h n -> p (h n)"), out_view[g]
+            else:
+                res = four.tile([P, 2 * QD], F32)
+                values, rows = y[:, part, :], out_last[part]
             nc.vector.tensor_scalar(
-                out=res[:],
-                in0=y[:].rearrange("p h n -> p (h n)"),
-                scalar1=mean[:],
-                scalar2=rstd[:],
-                op0=ALU.subtract,
-                op1=ALU.mult,
+                out=res[:], in0=values, scalar1=mean, scalar2=rstd[:], op0=ALU.subtract, op1=ALU.mult
             )
-            nc.sync.dma_start(out=out_view[g], in_=res[:])
+            nc.sync.dma_start(out=rows, in_=res[:])
 
         def in_range(g):
             return 0 <= g < GROUPS
 
-        for i in range(GROUPS + 4):
+        for i in range(GROUPS):
             if in_range(i + LOOKAHEAD):
                 load(i + LOOKAHEAD)
-            if in_range(i):
-                start_group(i)
-                transpose_x(i, 0)
-                transpose_x(i, 1)
-            if in_range(i - 1):
+            start_group(i)
+            transpose_x(i, 0)
+            transpose_x(i, 1)
+            if i >= 1:
                 quantise(i - 1, 1)
-            if in_range(i - 2):
+            if i >= 2:
                 add_bias(i - 2, 1)
-            if in_range(i - 4):
+            if i >= 4:
                 normalise_and_store(i - 4)
-            if in_range(i - 2):
+            if i >= 2:
                 product(i - 2, 1)
-            if in_range(i - 1):
+            if i >= 1:
                 multiply(i - 1, 0)
-            if in_range(i - 3):
+            if i >= 3:
                 sample_statistics(i - 3)
-            if in_range(i):
-                transpose_x(i, 2)
-                transpose_x(i, 3)
-                transpose_kv(i)
-            if in_range(i - 1):
+            transpose_x(i, 2)
+            transpose_x(i, 3)
+            transpose_kv(i)
+            if i >= 1:
                 add_bias(i - 1, 0)
-            if in_range(i - 3):
+            if i >= 3:
                 mean_of_sample(i - 3)
-            if in_range(i):
-                quantise(i, 0)
-            if in_range(i - 3):
+            quantise(i, 0)
+            if i >= 3:
                 minus_variance(i - 3)
-            if in_range(i - 1):
+            if i >= 1:
                 product(i - 1, 0)
-            if in_range(i - 3):
+            copy_kv(i)
+            if i >= 3:
                 inverse_deviation(i - 3)
-            if in_range(i - 2):
+            if i >= 2:
                 sum_of_squares(i - 2)
-            if in_range(i - 1):
+            if i >= 1:
                 multiply(i - 1, 1)
+
+        add_bias(LAST - 1, 1)
+        quantise(LAST, 1)
+        product(LAST - 1, 1)
+        multiply(LAST, 0)
+        multiply(LAST, 1)
+        sample_statistics(LAST - 2)
+        sum_of_squares(LAST - 1)
+        add_bias(LAST, 0)
+        normalise_and_store(LAST - 3)
+        product(LAST, 0)
+        sum_of_squares(LAST, 0)
+        add_bias(LAST, 1)
+        mean_of_sample(LAST - 2)
+        product(LAST, 1)
+        minus_variance(LAST - 2)
+        inverse_deviation(LAST - 2)
+        normalise_and_store(LAST - 2)
+        sample_statistics(LAST - 1)
+        sample_statistics(LAST, 0)
+        sum_of_squares(LAST, 1)
+        mean_of_sample(LAST - 1)
+        mean_of_sample(LAST, 0)
+        minus_variance(LAST - 1)
+        minus_variance(LAST, 0)
+        inverse_deviation(LAST - 1)
+        inverse_deviation(LAST, 0)
+        sample_statistics(LAST, 1)
+        normalise_and_store(LAST - 1)
+        normalise_and_store(LAST, 0)
+        mean_of_sample(LAST, 1)
+        minus_variance(LAST, 1)
+        inverse_deviation(LAST, 1)
+        normalise_and_store(LAST, 1)

@@ -152,8 +152,12 @@ def tile_parallelretention_pb_t_kernel(tc, x, Wq_words, Wq_scales, bq, kv, decay
 
         def transpose_kv(g):
             kvT_ps = psum_one.tile([P, S, P], BF16)
-            for j in range(S):
+            for j in range(2):
                 nc.tensor.transpose(kvT_ps[:, j, :], kv_tiles[g][:, j, :], ident_bf16[:])
+            for j in range(2, S):
+                nc.tensor.matmul(
+                    out=kvT_ps[:, j, :], lhsT=kv_tiles[g][:, j, :], rhs=ident_bf16[:], start=True, stop=True
+                )
             live[("kvT_ps", g)] = kvT_ps
 
         def copy_kv(g):

@@ -48,6 +48,7 @@ def tile_parallelretention_pb_t_kernel(tc, x, Wq_words, Wq_scales, bq, kv, decay
         kv_pool = ctx.enter_context(tc.tile_pool(name="kv_pool", bufs=GROUPS))
         two = ctx.enter_context(tc.tile_pool(name="two", bufs=2))
         four = ctx.enter_context(tc.tile_pool(name="four", bufs=4))
+        six = ctx.enter_context(tc.tile_pool(name="six", bufs=6))
         psum_x = ctx.enter_context(tc.psum_pool(name="psum_x", bufs=S))
         psum_one = ctx.enter_context(tc.psum_pool(name="psum_one", bufs=1))
         psum_half = ctx.enter_context(tc.psum_pool(name="psum_half", bufs=2))
@@ -85,12 +86,15 @@ def tile_parallelretention_pb_t_kernel(tc, x, Wq_words, Wq_scales, bq, kv, decay
         x_tiles = []
         kv_tiles = []
 
-        def load(g):
-            x_sb = x_pool.tile([P, S, E], BF16)
-            for j in range(S):
+        def load_x(g, blocks):
+            if blocks[0] == 0:
+                x_sb = x_pool.tile([P, S, E], BF16)
+                x_tiles.append(x_sb)
+            for j in blocks:
                 rows = x_view[g, :, j, :] if g < LAST else x_last[:, j // 2, j % 2, :]
-                nc.sync.dma_start(out=x_sb[:, j, :], in_=rows)
-            x_tiles.append(x_sb)
+                nc.sync.dma_start(out=x_tiles[g][:, j, :], in_=rows)
+
+        def load_kv(g):
             kv_sb = kv_pool.tile([P, S, QD], BF16)
             if g < LAST:
                 nc.sync.dma_start(out=kv_sb[:], in_=kv_view[g])
@@ -98,7 +102,12 @@ def tile_parallelretention_pb_t_kernel(tc, x, Wq_words, Wq_scales, bq, kv, decay
                 nc.sync.dma_start(out=kv_sb[:].rearrange("p (h j) k -> p h (j k)", h=2), in_=kv_last)
             kv_tiles.append(kv_sb)
 
+        def load(g):
+            load_x(g, range(S))
+            load_kv(g)
+
         load(0)
+        load_x(1, range(0, 2))
         w_words = const.tile([P, PASSES, 2 * QD], U8, align_bytes=64)
         nc.sync.dma_start(out=w_words[:].bitcast(I32), in_=Wq_words.bitcast(I32).rearrange("c p n -> p c n"))
         for quad in range(4):
@@ -106,7 +115,9 @@ def tile_parallelretention_pb_t_kernel(tc, x, Wq_words, Wq_scales, bq, kv, decay
                 out=w_planes[32 * quad : 32 * quad + 4].bitcast(I32),
                 in_=Wq_scales.bitcast(I32)[:, 4 * quad : 4 * quad + 4, :].rearrange("c r n -> r c n"),
             )
-        for g in range(1, LOOKAHEAD):
+        load_x(1, range(2, S))
+        load_kv(1)
+        for g in range(2, LOOKAHEAD):
             load(g)
 
         dT_ps = psum_one.tile([P, S, P], BF16, name="kvT_ps")
@@ -118,7 +129,7 @@ def tile_parallelretention_pb_t_kernel(tc, x, Wq_words, Wq_scales, bq, kv, decay
         bias = const.tile([P, QD], F32)
         nc.vector.tensor_copy(out=bias[:], in_=bias_ps[:, 0, 0, :])
 
-        stat_ps = psum_one.tile([P, GROUPS + 1, 4], F32)
+        stat_ps = psum_one.tile([P, GROUPS - 2, 4], F32)
 
         live = {}
 
@@ -235,31 +246,36 @@ def tile_parallelretention_pb_t_kernel(tc, x, Wq_words, Wq_scales, bq, kv, decay
 
         def sample_statistics(g, part=None):
             y, sums = live[("y", g)]
-            if part is None:
-                nc.tensor.matmul(out=stat_ps[:, g, 0:3], lhsT=sample_mean[:], rhs=sums[:, 0:3, 0], start=True, stop=True)
+            if g >= LAST - 1:
+                stat = psum_x.tile([P, 4], F32, name="xT_ps")
             else:
-                nc.tensor.matmul(
-                    out=stat_ps[:, g + part, 0:2], lhsT=half_mean[:], rhs=sums[:, part:4:2, 0], start=True, stop=True
-                )
+                stat = stat_ps[:, g, :]
+            live[("stat", g, part)] = stat
+            if part is None:
+                nc.tensor.matmul(out=stat[:, 0:3], lhsT=sample_mean[:], rhs=sums[:, 0:3, 0], start=True, stop=True)
+            else:
+                nc.tensor.matmul(out=stat[:, 0:2], lhsT=half_mean[:], rhs=sums[:, part:4:2, 0], start=True, stop=True)
 
         def mean_of_sample(g, part=None):
             if part is None:
+                stat = live[("stat", g, None)]
                 mean = four.tile([P, 1], F32)
                 nc.vector.tensor_scalar(
                     out=mean[:],
-                    in0=stat_ps[:, g, 0:1],
-                    scalar1=stat_ps[:, g, 1:2],
+                    in0=stat[:, 0:1],
+                    scalar1=stat[:, 1:2],
                     scalar2=1.0,
                     op0=ALU.add,
                     op1=ALU.mult,
                 )
                 live[("mean", g, part)] = mean[:]
             else:
-                live[("mean", g, part)] = stat_ps[:, g + part, 0:1]
+                live[("mean", g, part)] = live[("stat", g, part)][:, 0:1]
 
         def minus_variance(g, part=None):
             mean = live[("mean", g, part)]
-            mean_square = stat_ps[:, g, 2:3] if part is None else stat_ps[:, g + part, 1:2]
+            stat = live[("stat", g, part)]
+            mean_square = stat[:, 2:3] if part is None else stat[:, 1:2]
             minus_var = four.tile([P, 1], F32)
             nc.vector.tensor_scalar(
                 out=minus_var[:], in0=mean, scalar1=mean, scalar2=mean_square, op0=ALU.mult, op1=ALU.subtract
@@ -279,10 +295,10 @@ def tile_parallelretention_pb_t_kernel(tc, x, Wq_words, Wq_scales, bq, kv, decay
             rstd = live.pop(("rstd", g, part))
             mean = live.pop(("mean", g, part))
             if part is None:
-                res = four.tile([P, S * QD], F32)
+                res = six.tile([P, S * QD], F32)
                 values, rows = y[:].rearrange("p h n -> p (h n)"), out_view[g]
             else:
-                res = four.tile([P, 2 * QD], F32)
+                res = six.tile([P, 2 * QD], F32)
                 values, rows = y[:, part, :], out_last[part]
             nc.vector.tensor_scalar(
                 out=res[:], in0=values, scalar1=mean, scalar2=rstd[:], op0=ALU.subtract, op1=ALU.mult
@@ -323,43 +339,43 @@ def tile_parallelretention_pb_t_kernel(tc, x, Wq_words, Wq_scales, bq, kv, decay
             if i >= 1:
                 product(i - 1, 0)
             copy_kv(i)
-            if i >= 3:
-                inverse_deviation(i - 3)
             if i >= 2:
                 sum_of_squares(i - 2)
+            if i >= 3:
+                inverse_deviation(i - 3)
             if i >= 1:
                 multiply(i - 1, 1)
 
-        add_bias(LAST - 1, 1)
         quantise(LAST, 1)
-        product(LAST - 1, 1)
+        add_bias(LAST - 1, 1)
         multiply(LAST, 0)
         multiply(LAST, 1)
         sample_statistics(LAST - 2)
-        sum_of_squares(LAST - 1)
         add_bias(LAST, 0)
-        normalise_and_store(LAST - 3)
+        product(LAST - 1, 1)
+        sum_of_squares(LAST - 1)
+        add_bias(LAST, 1)
         product(LAST, 0)
         sum_of_squares(LAST, 0)
-        add_bias(LAST, 1)
-        mean_of_sample(LAST - 2)
         product(LAST, 1)
-        minus_variance(LAST - 2)
-        inverse_deviation(LAST - 2)
-        normalise_and_store(LAST - 2)
+        sum_of_squares(LAST, 1)
         sample_statistics(LAST - 1)
         sample_statistics(LAST, 0)
-        sum_of_squares(LAST, 1)
-        mean_of_sample(LAST - 1)
-        mean_of_sample(LAST, 0)
-        minus_variance(LAST - 1)
-        minus_variance(LAST, 0)
-        inverse_deviation(LAST - 1)
-        inverse_deviation(LAST, 0)
         sample_statistics(LAST, 1)
-        normalise_and_store(LAST - 1)
-        normalise_and_store(LAST, 0)
+        normalise_and_store(LAST - 3)
+        mean_of_sample(LAST - 2)
+        mean_of_sample(LAST - 1)
+        minus_variance(LAST - 2)
+        inverse_deviation(LAST - 2)
+        minus_variance(LAST - 1)
+        inverse_deviation(LAST - 1)
+        normalise_and_store(LAST - 2)
+        mean_of_sample(LAST, 0)
         mean_of_sample(LAST, 1)
+        minus_variance(LAST, 0)
+        inverse_deviation(LAST, 0)
         minus_variance(LAST, 1)
         inverse_deviation(LAST, 1)
+        normalise_and_store(LAST - 1)
+        normalise_and_store(LAST, 0)
         normalise_and_store(LAST, 1)

from contextlib import ExitStack

import concourse.mybir as mybir
from concourse.masks import make_identity

F32 = mybir.dt.float32
BF16 = mybir.dt.bfloat16
I32 = mybir.dt.int32
U32 = mybir.dt.uint32
U8 = mybir.dt.uint8
FP8X4 = mybir.dt.float8_e4m3fn_x4
FP4X4 = mybir.dt.float4_e2m1fn_x4
ALU = mybir.AluOpType
ACT = mybir.ActivationFunctionType

P = 128
SAMPLES = 64
L = 128
E = 1024
QD = 128
EPS = 1e-5
K_PASS = 512
PASSES = E // K_PASS
WORDS_PASS = K_PASS // 2
S = 4
GROUP_ROWS = P * S
GROUPS = SAMPLES * L // GROUP_ROWS
LAST = GROUPS - 1
LOOKAHEAD = 4

FLOPS = 2 * SAMPLES * L * E * QD + 2 * SAMPLES * L * QD * QD


def tile_parallelretention_pb_t_kernel(tc, x, Wq_words, Wq_scales, bq, kv, decay_mask, out):
    nc = tc.nc
    x_view = x.rearrange("b h l e -> (b h l) e").rearrange("(g p j) e -> g p j e", p=P, j=S)
    kv_view = kv.rearrange("b h l k -> (b h l) k").rearrange("(g p j) k -> g p j k", p=P, j=S)
    out_view = out.rearrange("b l q -> (b l) q").rearrange("(g p j) q -> g p (j q)", p=P, j=S)
    first_row = LAST * GROUP_ROWS
    x_last = x.rearrange("b h l e -> (b h l) e")[first_row:, :].rearrange("(h p j) e -> p h j e", p=P, j=2)
    kv_last = kv.rearrange("b h l k -> (b h l) k")[first_row:, :].rearrange("(h p j) k -> p h (j k)", p=P, j=2)
    out_last = out.rearrange("b l q -> (b l) q")[first_row:, :].rearrange("(h p j) q -> h p (j q)", p=P, j=2)

    with ExitStack() as ctx:
        ctx.enter_context(tc.manual_schedule())
        const = ctx.enter_context(tc.tile_pool(name="const", bufs=1))
        x_pool = ctx.enter_context(tc.tile_pool(name="x_pool", bufs=GROUPS))
        kv_pool = ctx.enter_context(tc.tile_pool(name="kv_pool", bufs=GROUPS))
        two = ctx.enter_context(tc.tile_pool(name="two", bufs=2))
        four = ctx.enter_context(tc.tile_pool(name="four", bufs=4))
        six = ctx.enter_context(tc.tile_pool(name="six", bufs=6))
        psum_x = ctx.enter_context(tc.psum_pool(name="psum_x", bufs=S))
        psum_one = ctx.enter_context(tc.psum_pool(name="psum_one", bufs=1))
        psum_half = ctx.enter_context(tc.psum_pool(name="psum_half", bufs=2))

        d_sb = const.tile([P, P], BF16)
        nc.scalar.dma_start(out=d_sb[:], in_=decay_mask.rearrange("o q k -> (o q) k"))
        bq_row = const.tile([P, QD], BF16)
        nc.gpsimd.memset(bq_row[:], 0.0)
        nc.scalar.dma_start(out=bq_row[0:1, :], in_=bq.rearrange("(o q) -> o q", o=1))
        ones = const.tile([P, P], BF16)
        nc.gpsimd.memset(ones[:], 1.0)

        w_planes = const.tile([P, PASSES, QD], U8, align_bytes=64)
        nc.vector.memset(w_planes[:].bitcast(I32), 0)
        eps = const.tile([P, 1], F32)
        nc.vector.memset(eps[:], EPS)
        sample_mean = const.tile([P, P], F32)
        nc.vector.memset(sample_mean[:], 0.0)
        for a in range(P // 32):
            rows = slice(32 * a, 32 * a + 32)
            nc.vector.memset(sample_mean[rows, rows], 1.0 / (L * QD))
        half_mean = const.tile([P, P], F32)
        nc.vector.memset(half_mean[:], 0.0)
        for a in range(2):
            rows = slice(64 * a, 64 * a + 64)
            nc.vector.memset(half_mean[rows, rows], 1.0 / (L * QD))
        ident_f32 = const.tile([P, P], F32)
        make_identity(nc, ident_f32[:])
        ident_bf16 = const.tile([P, P], BF16)
        make_identity(nc, ident_bf16[:])

        warm = const.tile([P, 1], F32)
        nc.scalar.activation(out=warm[:], in_=eps[:], func=ACT.Abs_reciprocal_sqrt)

        x_tiles = []
        kv_tiles = []

        def load_x(g, blocks):
            if blocks[0] == 0:
                x_sb = x_pool.tile([P, S, E], BF16)
                x_tiles.append(x_sb)
            for j in blocks:
                rows = x_view[g, :, j, :] if g < LAST else x_last[:, j // 2, j % 2, :]
                nc.sync.dma_start(out=x_tiles[g][:, j, :], in_=rows)

        def load_kv(g):
            kv_sb = kv_pool.tile([P, S, QD], BF16)
            if g < LAST:
                nc.sync.dma_start(out=kv_sb[:], in_=kv_view[g])
            else:
                nc.sync.dma_start(out=kv_sb[:].rearrange("p (h j) k -> p h (j k)", h=2), in_=kv_last)
            kv_tiles.append(kv_sb)

        def load(g):
            load_x(g, range(S))
            load_kv(g)

        load(0)
        load_x(1, range(0, 2))
        w_words = const.tile([P, PASSES, 2 * QD], U8, align_bytes=64)
        nc.sync.dma_start(out=w_words[:].bitcast(I32), in_=Wq_words.bitcast(I32).rearrange("c p n -> p c n"))
        for quad in range(4):
            nc.sync.dma_start(
                out=w_planes[32 * quad : 32 * quad + 4].bitcast(I32),
                in_=Wq_scales.bitcast(I32)[:, 4 * quad : 4 * quad + 4, :].rearrange("c r n -> r c n"),
            )
        load_x(1, range(2, S))
        load_kv(1)
        for g in range(2, LOOKAHEAD):
            load(g)

        dT_ps = psum_one.tile([P, S, P], BF16, name="kvT_ps")
        nc.tensor.transpose(dT_ps[:, 0, :], d_sb[:], ident_bf16[:])
        dT = const.tile([P, QD], BF16)
        nc.vector.tensor_copy(out=dT[:], in_=dT_ps[:, 0, :])
        bias_ps = psum_half.tile([P, 2, 2, QD], F32, name="qg_ps")
        nc.tensor.matmul(out=bias_ps[:, 0, 0, :], lhsT=ones[:], rhs=bq_row[:], start=True, stop=True)
        bias = const.tile([P, QD], F32)
        nc.vector.tensor_copy(out=bias[:], in_=bias_ps[:, 0, 0, :])

        stat_ps = psum_one.tile([P, GROUPS - 2, 4], F32)

        live = {}

        def start_group(g):
            grouped = two.tile([P, S, PASSES, P, 4], BF16, align_bytes=64)
            codes = two.tile([P, S, PASSES, P], U32, align_bytes=64)
            planes = two.tile([P, S, PASSES, P], U8, align_bytes=64)
            live[("x", g)] = (grouped, codes, planes)

        def transpose_x(g, j):
            grouped, codes, planes = live[("x", g)]
            xT_ps = psum_x.tile([P, PASSES, 2, P], F32)
            words = x_tiles[g][:, j, :].bitcast(F32)
            for c in range(PASSES):
                for u in range(2):
                    nc.tensor.transpose(
                        xT_ps[:, c, u, :],
                        words[:, WORDS_PASS * c + u : WORDS_PASS * (c + 1) : 2],
                        ident_f32[:],
                    )
            nc.scalar.copy(out=grouped[:, j].bitcast(F32), in_=xT_ps[:].rearrange("p c u r -> p c r u"))

        def quantise(g, half):
            grouped, codes, planes = live[("x", g)]
            blocks = slice(2 * half, 2 * half + 2)
            nc.vector.quantize_mx(
                out=codes[:, blocks].rearrange("p j c r -> p (j c r)").bitcast(FP8X4),
                scales=planes[:, blocks].rearrange("p j c r -> p (j c r)"),
                in_=grouped[:, blocks].rearrange("p j c r t -> p (j c r t)"),
            )

        def transpose_kv(g):
            kvT_ps = psum_one.tile([P, S, P], BF16)
            for j in range(2):
                nc.tensor.transpose(kvT_ps[:, j, :], kv_tiles[g][:, j, :], ident_bf16[:])
            for j in range(2, S):
                nc.tensor.matmul(
                    out=kvT_ps[:, j, :], lhsT=kv_tiles[g][:, j, :], rhs=ident_bf16[:], start=True, stop=True
                )
            live[("kvT_ps", g)] = kvT_ps

        def copy_kv(g):
            kvT_ps = live.pop(("kvT_ps", g))
            kvT = two.tile([P, S, P], BF16)
            if g % 2 == 0:
                nc.vector.tensor_copy(out=kvT[:], in_=kvT_ps[:])
            else:
                nc.scalar.copy(out=kvT[:], in_=kvT_ps[:])
            live[("kvT", g)] = kvT

        def multiply(g, half):
            grouped, codes, planes = live[("x", g)]
            kvT = live[("kvT", g)]
            if g == LAST and half == 1:
                qg_ps = psum_x.tile([P, 2, 2, QD], F32, name="xT_ps")
            else:
                qg_ps = psum_half.tile([P, 2, 2, QD], F32)
            for b in range(2):
                j = 2 * half + b
                for c in range(PASSES):
                    nc.tensor.matmul_mx(
                        out=qg_ps[:, 0, b, :],
                        lhsT=codes[:, j, c, :].bitcast(FP8X4),
                        lhsT_scale=planes[:, j, c, :],
                        rhs=w_words[:, c, :].bitcast(FP4X4),
                        rhs_scale=w_planes[:, c, :],
                        start=(c == 0),
                        stop=(c == PASSES - 1),
                    )
            for b in range(2):
                nc.tensor.matmul(out=qg_ps[:, 1, b, :], lhsT=kvT[:, 2 * half + b, :], rhs=dT[:], start=True, stop=True)
            live[("qg", g, half)] = qg_ps

        def add_bias(g, half):
            qg_ps = live[("qg", g, half)]
            if half == 0:
                biased = two.tile([P, 2, 2, QD], F32)
                live[("biased", g)] = biased
            biased = live[("biased", g)]
            nc.vector.tensor_tensor(
                out=biased[:, half], in0=qg_ps[:, 0], in1=bias[:].unsqueeze(1).to_broadcast([P, 2, QD]), op=ALU.add
            )

        def product(g, half):
            qg_ps = live.pop(("qg", g, half))
            biased = live[("biased", g)]
            if half == 0:
                y = four.tile([P, 2, 2 * QD], F32)
                sums = four.tile([P, 4, 8], F32)
                live[("y", g)] = (y, sums)
            y, sums = live[("y", g)]
            nc.vector.scalar_tensor_tensor(
                out=y[:, half, :],
                in0=qg_ps[:, 1].rearrange("p b q -> p (b q)"),
                scalar=1.0,
                in1=biased[:, half].rearrange("p b q -> p (b q)"),
                op0=ALU.mult,
                op1=ALU.mult,
                accum_out=sums[:, half, 0:1],
            )

        def sum_of_squares(g, part=None):
            y, sums = live[("y", g)]
            if part is None:
                squares = two.tile([P, S * QD], F32)
                nc.scalar.activation(
                    out=squares[:], in_=y[:].rearrange("p h n -> p (h n)"), func=ACT.Square, accum_out=sums[:, 2, 0:1]
                )
            else:
                squares = two.tile([P, 2 * QD], F32)
                nc.scalar.activation(
                    out=squares[:], in_=y[:, part, :], func=ACT.Square, accum_out=sums[:, 2 + part, 0:1]
                )

        def sample_statistics(g, part=None):
            y, sums = live[("y", g)]
            if g >= LAST - 1:
                stat = psum_x.tile([P, 4], F32, name="xT_ps")
            else:
                stat = stat_ps[:, g, :]
            live[("stat", g, part)] = stat
            if part is None:
                nc.tensor.matmul(out=stat[:, 0:3], lhsT=sample_mean[:], rhs=sums[:, 0:3, 0], start=True, stop=True)
            else:
                nc.tensor.matmul(out=stat[:, 0:2], lhsT=half_mean[:], rhs=sums[:, part:4:2, 0], start=True, stop=True)

        def mean_of_sample(g, part=None):
            if part is None:
                stat = live[("stat", g, None)]
                mean = four.tile([P, 1], F32)
                nc.vector.tensor_scalar(
                    out=mean[:],
                    in0=stat[:, 0:1],
                    scalar1=stat[:, 1:2],
                    scalar2=1.0,
                    op0=ALU.add,
                    op1=ALU.mult,
                )
                live[("mean", g, part)] = mean[:]
            else:
                live[("mean", g, part)] = live[("stat", g, part)][:, 0:1]

        def minus_variance(g, part=None):
            mean = live[("mean", g, part)]
            stat = live[("stat", g, part)]
            mean_square = stat[:, 2:3] if part is None else stat[:, 1:2]
            minus_var = four.tile([P, 1], F32)
            nc.vector.tensor_scalar(
                out=minus_var[:], in0=mean, scalar1=mean, scalar2=mean_square, op0=ALU.mult, op1=ALU.subtract
            )
            live[("minus_var", g, part)] = minus_var

        def inverse_deviation(g, part=None):
            minus_var = live.pop(("minus_var", g, part))
            rstd = four.tile([P, 1], F32)
            nc.scalar.activation(
                out=rstd[:], in_=minus_var[:], func=ACT.Abs_reciprocal_sqrt, bias=eps[:], scale=-1.0
            )
            live[("rstd", g, part)] = rstd

        def normalise_and_store(g, part=None):
            y, sums = live[("y", g)]
            rstd = live.pop(("rstd", g, part))
            mean = live.pop(("mean", g, part))
            if part is None:
                res = six.tile([P, S * QD], F32)
                values, rows = y[:].rearrange("p h n -> p (h n)"), out_view[g]
            else:
                res = six.tile([P, 2 * QD], F32)
                values, rows = y[:, part, :], out_last[part]
            nc.vector.tensor_scalar(
                out=res[:], in0=values, scalar1=mean, scalar2=rstd[:], op0=ALU.subtract, op1=ALU.mult
            )
            nc.sync.dma_start(out=rows, in_=res[:])

        def in_range(g):
            return 0 <= g < GROUPS

        for i in range(GROUPS):
            if in_range(i + LOOKAHEAD):
                load(i + LOOKAHEAD)
            start_group(i)
            transpose_x(i, 0)
            transpose_x(i, 1)
            if i >= 1:
                quantise(i - 1, 1)
            if i >= 2:
                add_bias(i - 2, 1)
            if i >= 4:
                normalise_and_store(i - 4)
            if i >= 2:
                product(i - 2, 1)
            if i >= 1:
                multiply(i - 1, 0)
            if i >= 3:
                sample_statistics(i - 3)
            transpose_x(i, 2)
            transpose_x(i, 3)
            transpose_kv(i)
            if i >= 1:
                add_bias(i - 1, 0)
            if i >= 3:
                mean_of_sample(i - 3)
            quantise(i, 0)
            if i >= 3:
                minus_variance(i - 3)
            if i >= 1:
                product(i - 1, 0)
            copy_kv(i)
            if i >= 2:
                sum_of_squares(i - 2)
            if i >= 3:
                inverse_deviation(i - 3)
            if i >= 1:
                multiply(i - 1, 1)

        quantise(LAST, 1)
        add_bias(LAST - 1, 1)
        multiply(LAST, 0)
        multiply(LAST, 1)
        sample_statistics(LAST - 2)
        add_bias(LAST, 0)
        product(LAST - 1, 1)
        sum_of_squares(LAST - 1)
        add_bias(LAST, 1)
        product(LAST, 0)
        sum_of_squares(LAST, 0)
        product(LAST, 1)
        sum_of_squares(LAST, 1)
        sample_statistics(LAST - 1)
        sample_statistics(LAST, 0)
        sample_statistics(LAST, 1)
        normalise_and_store(LAST - 3)
        mean_of_sample(LAST - 2)
        mean_of_sample(LAST - 1)
        minus_variance(LAST - 2)
        inverse_deviation(LAST - 2)
        minus_variance(LAST - 1)
        inverse_deviation(LAST - 1)
        normalise_and_store(LAST - 2)
        mean_of_sample(LAST, 0)
        mean_of_sample(LAST, 1)
        minus_variance(LAST, 0)
        inverse_deviation(LAST, 0)
        minus_variance(LAST, 1)
        inverse_deviation(LAST, 1)
        normalise_and_store(LAST - 1)
        normalise_and_store(LAST, 0)
        normalise_and_store(LAST, 1)
